import numpy as np
import ml_dtypes

BF16 = ml_dtypes.bfloat16


def bf(x):
    return np.asarray(x, np.float32).astype(BF16)


def f32(x):
    return np.asarray(x, np.float32)


def f64(x):
    return np.asarray(x).astype(np.float64)


def striped(idx):
    return np.tile(idx.reshape(-1, 16).T, (8, 1))


S, D, M, N = 4096, 128, 128, 2048


def setup_inputs():
    return {
        "table": bf(np.random.standard_normal((D, S))),
        "w0": bf(np.random.standard_normal((D, M)) / np.sqrt(D)),
        "w1": bf(np.random.standard_normal((D, M)) / np.sqrt(D)),
        "w2": bf(np.random.standard_normal((D, M)) / np.sqrt(D)),
        "b0": f32(0.1 * np.random.standard_normal((M, 1))),
        "b1": f32(0.1 * np.random.standard_normal((M, 1))),
        "b2": f32(0.1 * np.random.standard_normal((M, 1))),
        "wa": bf(np.random.standard_normal((M, 1)) / np.sqrt(M)),
        "offs": striped(np.random.permutation(np.tile(np.arange(S), 2))[:N]),
    }


def reference(table, w0, w1, w2, b0, b1, b2, wa, offs):
    idx = offs[:16].T.reshape(-1)
    e = f64(table)[:, idx]
    p = np.stack([f64(w0).T @ e + f64(b0), f64(w1).T @ e + f64(b1), f64(w2).T @ e + f64(b2)])
    l = np.einsum("nmt,m->nt", p, f64(wa)[:, 0])
    a = np.exp(l - l.max(axis=0, keepdims=True))
    a = a / a.sum(axis=0, keepdims=True)
    return (p * a[:, None, :]).sum(axis=0)

@@ -1,0 +1,135 @@
+import concourse.mybir as mybir
+from concourse.masks import make_identity
+
+BF16, F32, U16 = mybir.dt.bfloat16, mybir.dt.float32, mybir.dt.uint16
+FUNC = mybir.ActivationFunctionType
+ALU = mybir.AluOpType
+AXIS = mybir.AxisListType
+
+P = 128
+WORDS = 4096
+TOKENS = 2048
+PROJS = 3
+PIECE = 512
+BLOCK = 128
+BLOCKS = PIECE // BLOCK
+PIECES = TOKENS // PIECE
+TABLE_LOADS = 4
+
+FLOPS = 2 * TOKENS * PROJS * (P * P + P)
+
+
+def tile_dynamicmetaembedding_kernel(tc, table, w0, w1, w2, b0, b1, b2, wa, offs, out):
+    nc = tc.nc
+    with (
+        tc.tile_pool(name="held", bufs=1) as held,
+        tc.tile_pool(name="work", bufs=2) as work,
+        tc.tile_pool(name="small", bufs=2) as small,
+    ):
+        offsets = held.tile([P, TOKENS // 16], U16, name="offsets")
+        nc.sync.dma_start(offsets[:], offs)
+
+        w_sb = []
+        for n, w in enumerate((w0, w1, w2)):
+            w_tile = held.tile([P, P], BF16, name=f"w{n}_sb")
+            nc.scalar.dma_start(w_tile[:], w)
+            w_sb.append(w_tile)
+
+        table_sb = held.tile([P, WORDS], BF16, name="table_sb")
+        span = WORDS // TABLE_LOADS
+        for part in range(TABLE_LOADS):
+            queue = nc.sync if part % 2 == 0 else nc.scalar
+            queue.dma_start(
+                table_sb[:, part * span : (part + 1) * span], table[:, part * span : (part + 1) * span]
+            )
+
+        b_sb = []
+        for n, b in enumerate((b0, b1, b2)):
+            b_tile = held.tile([P, 1], F32, name=f"b{n}_sb")
+            nc.sync.dma_start(b_tile[:], b)
+            b_sb.append(b_tile)
+        wa_sb = held.tile([P, 1], BF16, name="wa_sb")
+        nc.scalar.dma_start(wa_sb[:], wa)
+
+        identity = held.tile([P, P], F32, name="identity")
+        make_identity(nc, identity[:])
+
+        p_f32, p_bf16 = [], []
+        with tc.psum_pool(name="proj_banks", bufs=8) as proj_banks:
+            for piece in range(PIECES):
+                piece_offsets = offsets[:, piece * (PIECE // 16) : (piece + 1) * (PIECE // 16)]
+                for n in range(PROJS):
+                    proj = proj_banks.tile([P, PIECE], F32, name="proj")
+                    nc.tensor.matmul(
+                        proj[:], w_sb[n][:], table_sb[:].indirect(piece_offsets), start=True, stop=True
+                    )
+                    exact = held.tile([P, PIECE], F32, name=f"p{n}_f32_{piece}")
+                    nc.scalar.activation(exact[:], proj[:], FUNC.Identity, bias=b_sb[n][:])
+                    p_f32.append(exact)
+                    rounded = held.tile([P, PIECE], BF16, name=f"p{n}_bf16_{piece}")
+                    nc.vector.tensor_copy(rounded[:], exact[:])
+                    p_bf16.append(rounded)
+
+        with (
+            tc.psum_pool(name="logit_banks", bufs=2) as logit_banks,
+            tc.psum_pool(name="spread_banks", bufs=6) as spread_banks,
+        ):
+            for piece in range(PIECES):
+                logits = logit_banks.tile([P, BLOCKS * PROJS], F32, name="logits")
+                for n in range(PROJS):
+                    for block in range(BLOCKS):
+                        column = block * PROJS + n
+                        nc.tensor.matmul(
+                            logits[:, column : column + 1],
+                            p_bf16[piece * PROJS + n][:, block * BLOCK : (block + 1) * BLOCK],
+                            wa_sb[:],
+                            start=True,
+                            stop=True,
+                        )
+
+                by_token = [P, BLOCKS, PROJS]
+                top = small.tile([P, BLOCKS], F32, name="top")
+                nc.vector.tensor_reduce(
+                    top[:], logits[:].rearrange("p (b n) -> p b n", n=PROJS), AXIS.X, ALU.max
+                )
+                shifted = small.tile([P, BLOCKS * PROJS], F32, name="shifted")
+                nc.vector.tensor_tensor(
+                    shifted[:].rearrange("p (b n) -> p b n", n=PROJS),
+                    logits[:].rearrange("p (b n) -> p b n", n=PROJS),
+                    top[:].unsqueeze(2).to_broadcast(by_token),
+                    ALU.subtract,
+                )
+                grown = small.tile([P, BLOCKS * PROJS], F32, name="grown")
+                nc.scalar.activation(grown[:], shifted[:], FUNC.Exp)
+                total = small.tile([P, BLOCKS], F32, name="total")
+                nc.vector.tensor_reduce(
+                    total[:], grown[:].rearrange("p (b n) -> p b n", n=PROJS), AXIS.X, ALU.add
+                )
+                inverse = small.tile([P, BLOCKS], F32, name="inverse")
+                nc.vector.reciprocal(inverse[:], total[:])
+                attn = small.tile([P, BLOCKS * PROJS], F32, name="attn")
+                nc.vector.tensor_tensor(
+                    attn[:].rearrange("p (b n) -> p b n", n=PROJS),
+                    grown[:].rearrange("p (b n) -> p b n", n=PROJS),
+                    inverse[:].unsqueeze(2).to_broadcast(by_token),
+                    ALU.mult,
+                )
+
+                terms = []
+                for n in range(PROJS):
+                    spread = spread_banks.tile([P, PIECE], F32, name="spread")
+                    for block in range(BLOCKS):
+                        column = block * PROJS + n
+                        nc.tensor.transpose(
+                            spread[:, block * BLOCK : (block + 1) * BLOCK],
+                            attn[:, column : column + 1].to_broadcast([P, P]),
+                            identity[:],
+                        )
+                    term = work.tile([P, PIECE], F32, name=f"term{n}")
+                    nc.vector.tensor_tensor(term[:], spread[:], p_f32[piece * PROJS + n][:], ALU.mult)
+                    terms.append(term)
+                first_two = work.tile([P, PIECE], F32, name="first_two")
+                nc.vector.tensor_tensor(first_two[:], terms[0][:], terms[1][:], ALU.add)
+                mixed = work.tile([P, PIECE], F32, name="mixed")
+                nc.vector.tensor_tensor(mixed[:], first_two[:], terms[2][:], ALU.add)
+                nc.sync.dma_start(out[:, piece * PIECE : (piece + 1) * PIECE], mixed[:])

@@ -10,6 +10,8 @@ P = 128
 WORDS = 4096
 TOKENS = 2048
 PROJS = 3
+LAST = 2
+OTHERS = (0, 1)
 PIECE = 512
 BLOCK = 128
 BLOCKS = PIECE // BLOCK
@@ -54,21 +56,32 @@ def tile_dynamicmetaembedding_kernel(tc, table, w0, w1, w2, b0, b1, b2, wa, offs
         identity = held.tile([P, P], F32, name="identity")
         make_identity(nc, identity[:])
 
-        p_f32, p_bf16 = [], []
+        p_last, p_gap, p_bf16 = [], [], []
         with tc.psum_pool(name="proj_banks", bufs=8) as proj_banks:
             for piece in range(PIECES):
                 piece_offsets = offsets[:, piece * (PIECE // 16) : (piece + 1) * (PIECE // 16)]
-                for n in range(PROJS):
-                    proj = proj_banks.tile([P, PIECE], F32, name="proj")
+                proj = {}
+                for n in (LAST,) + OTHERS:
+                    proj[n] = proj_banks.tile([P, PIECE], F32, name="proj")
                     nc.tensor.matmul(
-                        proj[:], w_sb[n][:], table_sb[:].indirect(piece_offsets), start=True, stop=True
+                        proj[n][:], w_sb[n][:], table_sb[:].indirect(piece_offsets), start=True, stop=True
                     )
-                    exact = held.tile([P, PIECE], F32, name=f"p{n}_f32_{piece}")
-                    nc.scalar.activation(exact[:], proj[:], FUNC.Identity, bias=b_sb[n][:])
-                    p_f32.append(exact)
-                    rounded = held.tile([P, PIECE], BF16, name=f"p{n}_bf16_{piece}")
-                    nc.vector.tensor_copy(rounded[:], exact[:])
-                    p_bf16.append(rounded)
+                rounded = {n: held.tile([P, PIECE], BF16, name=f"p{n}_bf16_{piece}") for n in range(PROJS)}
+                p_bf16.append(rounded)
+
+                last = held.tile([P, PIECE], F32, name=f"p_last_{piece}")
+                nc.scalar.activation(last[:], proj[LAST][:], FUNC.Identity, bias=b_sb[LAST][:])
+                nc.vector.tensor_copy(rounded[LAST][:], last[:])
+                p_last.append(last)
+
+                gaps = {}
+                for n in OTHERS:
+                    nc.scalar.activation(rounded[n][:], proj[n][:], FUNC.Identity, bias=b_sb[n][:])
+                    gaps[n] = held.tile([P, PIECE], F32, name=f"p_gap{n}_{piece}")
+                    nc.vector.scalar_tensor_tensor(
+                        gaps[n][:], proj[n][:], b_sb[n][:], last[:], ALU.add, ALU.subtract
+                    )
+                p_gap.append(gaps)
 
         with (
             tc.psum_pool(name="logit_banks", bufs=2) as logit_banks,
@@ -81,7 +94,7 @@ def tile_dynamicmetaembedding_kernel(tc, table, w0, w1, w2, b0, b1, b2, wa, offs
                         column = block * PROJS + n
                         nc.tensor.matmul(
                             logits[:, column : column + 1],
-                            p_bf16[piece * PROJS + n][:, block * BLOCK : (block + 1) * BLOCK],
+                            p_bf16[piece][n][:, block * BLOCK : (block + 1) * BLOCK],
                             wa_sb[:],
                             start=True,
                             stop=True,
@@ -115,8 +128,8 @@ def tile_dynamicmetaembedding_kernel(tc, table, w0, w1, w2, b0, b1, b2, wa, offs
                     ALU.mult,
                 )
 
-                terms = []
-                for n in range(PROJS):
+                mixed = p_last[piece]
+                for n in OTHERS:
                     spread = spread_banks.tile([P, PIECE], F32, name="spread")
                     for block in range(BLOCKS):
                         column = block * PROJS + n
@@ -126,10 +139,8 @@ def tile_dynamicmetaembedding_kernel(tc, table, w0, w1, w2, b0, b1, b2, wa, offs
                             identity[:],
                         )
                     term = work.tile([P, PIECE], F32, name=f"term{n}")
-                    nc.vector.tensor_tensor(term[:], spread[:], p_f32[piece * PROJS + n][:], ALU.mult)
-                    terms.append(term)
-                first_two = work.tile([P, PIECE], F32, name="first_two")
-                nc.vector.tensor_tensor(first_two[:], terms[0][:], terms[1][:], ALU.add)
-                mixed = work.tile([P, PIECE], F32, name="mixed")
-                nc.vector.tensor_tensor(mixed[:], first_two[:], terms[2][:], ALU.add)
+                    nc.vector.tensor_tensor(term[:], spread[:], p_gap[piece][n][:], ALU.mult)
+                    partial = work.tile([P, PIECE], F32, name=f"partial{n}")
+                    nc.vector.tensor_tensor(partial[:], mixed[:], term[:], ALU.add)
+                    mixed = partial
                 nc.sync.dma_start(out[:, piece * PIECE : (piece + 1) * PIECE], mixed[:])

@@ -27,6 +27,7 @@ def tile_dynamicmetaembedding_kernel(tc, table, w0, w1, w2, b0, b1, b2, wa, offs
         tc.tile_pool(name="held", bufs=1) as held,
         tc.tile_pool(name="work", bufs=2) as work,
         tc.tile_pool(name="small", bufs=2) as small,
+        tc.psum_pool(name="logit_banks", bufs=2) as logit_banks,
     ):
         offsets = held.tile([P, TOKENS // 16], U16, name="offsets")
         nc.sync.dma_start(offsets[:], offs)
@@ -56,8 +57,13 @@ def tile_dynamicmetaembedding_kernel(tc, table, w0, w1, w2, b0, b1, b2, wa, offs
         identity = held.tile([P, P], F32, name="identity")
         make_identity(nc, identity[:])
 
-        p_last, p_gap, p_bf16 = [], [], []
-        with tc.psum_pool(name="proj_banks", bufs=8) as proj_banks:
+        zero = held.tile([P, 1], F32, name="zero")
+        nc.vector.memset(zero[:], 0.0)
+        one = held.tile([P, 1], F32, name="one")
+        nc.scalar.activation(one[:], zero[:], FUNC.Exp)
+
+        p_last, gap_f32, gap_bf16 = [], [], []
+        with tc.psum_pool(name="proj_banks", bufs=6) as proj_banks:
             for piece in range(PIECES):
                 piece_offsets = offsets[:, piece * (PIECE // 16) : (piece + 1) * (PIECE // 16)]
                 proj = {}
@@ -66,65 +72,63 @@ def tile_dynamicmetaembedding_kernel(tc, table, w0, w1, w2, b0, b1, b2, wa, offs
                     nc.tensor.matmul(
                         proj[n][:], w_sb[n][:], table_sb[:].indirect(piece_offsets), start=True, stop=True
                     )
-                rounded = {n: held.tile([P, PIECE], BF16, name=f"p{n}_bf16_{piece}") for n in range(PROJS)}
-                p_bf16.append(rounded)
 
                 last = held.tile([P, PIECE], F32, name=f"p_last_{piece}")
                 nc.scalar.activation(last[:], proj[LAST][:], FUNC.Identity, bias=b_sb[LAST][:])
-                nc.vector.tensor_copy(rounded[LAST][:], last[:])
                 p_last.append(last)
 
-                gaps = {}
+                exact, rounded = {}, {}
                 for n in OTHERS:
-                    nc.scalar.activation(rounded[n][:], proj[n][:], FUNC.Identity, bias=b_sb[n][:])
-                    gaps[n] = held.tile([P, PIECE], F32, name=f"p_gap{n}_{piece}")
+                    exact[n] = held.tile([P, PIECE], F32, name=f"gap{n}_f32_{piece}")
                     nc.vector.scalar_tensor_tensor(
-                        gaps[n][:], proj[n][:], b_sb[n][:], last[:], ALU.add, ALU.subtract
+                        exact[n][:], proj[n][:], b_sb[n][:], last[:], ALU.add, ALU.subtract
                     )
-                p_gap.append(gaps)
+                    rounded[n] = held.tile([P, PIECE], BF16, name=f"gap{n}_bf16_{piece}")
+                nc.scalar.activation(rounded[0][:], exact[0][:], FUNC.Copy)
+                nc.vector.tensor_copy(rounded[1][:], exact[1][:])
+                gap_f32.append(exact)
+                gap_bf16.append(rounded)
 
-        with (
-            tc.psum_pool(name="logit_banks", bufs=2) as logit_banks,
-            tc.psum_pool(name="spread_banks", bufs=6) as spread_banks,
-        ):
+        with tc.psum_pool(name="spread_banks", bufs=6) as spread_banks:
             for piece in range(PIECES):
-                logits = logit_banks.tile([P, BLOCKS * PROJS], F32, name="logits")
-                for n in range(PROJS):
+                logits = logit_banks.tile([P, BLOCKS * len(OTHERS)], F32, name="logits")
+                for n in OTHERS:
                     for block in range(BLOCKS):
-                        column = block * PROJS + n
+                        column = block * len(OTHERS) + n
                         nc.tensor.matmul(
                             logits[:, column : column + 1],
-                            p_bf16[piece][n][:, block * BLOCK : (block + 1) * BLOCK],
+                            gap_bf16[piece][n][:, block * BLOCK : (block + 1) * BLOCK],
                             wa_sb[:],
                             start=True,
                             stop=True,
                         )
+                logits_by_token = logits[:].rearrange("p (b n) -> p b n", n=len(OTHERS))
 
-                by_token = [P, BLOCKS, PROJS]
                 top = small.tile([P, BLOCKS], F32, name="top")
-                nc.vector.tensor_reduce(
-                    top[:], logits[:].rearrange("p (b n) -> p b n", n=PROJS), AXIS.X, ALU.max
-                )
+                nc.vector.tensor_reduce(top[:], logits_by_token, AXIS.X, ALU.max)
                 shifted = small.tile([P, BLOCKS * PROJS], F32, name="shifted")
+                shifted_by_token = shifted[:].rearrange("p (b n) -> p b n", n=PROJS)
+                nc.vector.tensor_scalar(
+                    shifted_by_token[:, :, LAST : LAST + 1], top[:].unsqueeze(2), 0.0, -1.0, ALU.max, ALU.mult
+                )
                 nc.vector.tensor_tensor(
-                    shifted[:].rearrange("p (b n) -> p b n", n=PROJS),
-                    logits[:].rearrange("p (b n) -> p b n", n=PROJS),
-                    top[:].unsqueeze(2).to_broadcast(by_token),
-                    ALU.subtract,
+                    shifted_by_token[:, :, 0:LAST],
+                    logits_by_token,
+                    shifted_by_token[:, :, LAST : LAST + 1].to_broadcast([P, BLOCKS, len(OTHERS)]),
+                    ALU.add,
                 )
                 grown = small.tile([P, BLOCKS * PROJS], F32, name="grown")
                 nc.scalar.activation(grown[:], shifted[:], FUNC.Exp)
+                grown_by_token = grown[:].rearrange("p (b n) -> p b n", n=PROJS)
                 total = small.tile([P, BLOCKS], F32, name="total")
-                nc.vector.tensor_reduce(
-                    total[:], grown[:].rearrange("p (b n) -> p b n", n=PROJS), AXIS.X, ALU.add
-                )
+                nc.vector.tensor_reduce(total[:], grown_by_token, AXIS.X, ALU.add)
                 inverse = small.tile([P, BLOCKS], F32, name="inverse")
                 nc.vector.reciprocal(inverse[:], total[:])
-                attn = small.tile([P, BLOCKS * PROJS], F32, name="attn")
+                attn = small.tile([P, BLOCKS * len(OTHERS)], F32, name="attn")
                 nc.vector.tensor_tensor(
-                    attn[:].rearrange("p (b n) -> p b n", n=PROJS),
-                    grown[:].rearrange("p (b n) -> p b n", n=PROJS),
-                    inverse[:].unsqueeze(2).to_broadcast(by_token),
+                    attn[:].rearrange("p (b n) -> p b n", n=len(OTHERS)),
+                    grown_by_token[:, :, 0:LAST],
+                    inverse[:].unsqueeze(2).to_broadcast([P, BLOCKS, len(OTHERS)]),
                     ALU.mult,
                 )
 
@@ -132,14 +136,14 @@ def tile_dynamicmetaembedding_kernel(tc, table, w0, w1, w2, b0, b1, b2, wa, offs
                 for n in OTHERS:
                     spread = spread_banks.tile([P, PIECE], F32, name="spread")
                     for block in range(BLOCKS):
-                        column = block * PROJS + n
+                        column = block * len(OTHERS) + n
                         nc.tensor.transpose(
                             spread[:, block * BLOCK : (block + 1) * BLOCK],
                             attn[:, column : column + 1].to_broadcast([P, P]),
                             identity[:],
                         )
                     term = work.tile([P, PIECE], F32, name=f"term{n}")
-                    nc.vector.tensor_tensor(term[:], spread[:], p_gap[piece][n][:], ALU.mult)
+                    nc.vector.tensor_tensor(term[:], spread[:], gap_f32[piece][n][:], ALU.mult)
                     partial = work.tile([P, PIECE], F32, name=f"partial{n}")
                     nc.vector.tensor_tensor(partial[:], mixed[:], term[:], ALU.add)
                     mixed = partial

@@ -14,7 +14,8 @@ LAST = 2
 OTHERS = (0, 1)
 PIECE = 512
 BLOCK = 128
-BLOCKS = PIECE // BLOCK
+BLOCKS = TOKENS // BLOCK
+BLOCKS_IN_PIECE = PIECE // BLOCK
 PIECES = TOKENS // PIECE
 TABLE_LOADS = 4
 
@@ -26,8 +27,7 @@ def tile_dynamicmetaembedding_kernel(tc, table, w0, w1, w2, b0, b1, b2, wa, offs
     with (
         tc.tile_pool(name="held", bufs=1) as held,
         tc.tile_pool(name="work", bufs=2) as work,
-        tc.tile_pool(name="small", bufs=2) as small,
-        tc.psum_pool(name="logit_banks", bufs=2) as logit_banks,
+        tc.psum_pool(name="logit_banks", bufs=1) as logit_banks,
     ):
         offsets = held.tile([P, TOKENS // 16], U16, name="offsets")
         nc.sync.dma_start(offsets[:], offs)
@@ -89,62 +89,64 @@ def tile_dynamicmetaembedding_kernel(tc, table, w0, w1, w2, b0, b1, b2, wa, offs
                 gap_f32.append(exact)
                 gap_bf16.append(rounded)
 
+        logits = logit_banks.tile([P, BLOCKS * len(OTHERS)], F32, name="logits")
+        for block in range(BLOCKS):
+            piece, block_in_piece = divmod(block, BLOCKS_IN_PIECE)
+            for n in OTHERS:
+                column = block * len(OTHERS) + n
+                nc.tensor.matmul(
+                    logits[:, column : column + 1],
+                    gap_bf16[piece][n][:, block_in_piece * BLOCK : (block_in_piece + 1) * BLOCK],
+                    wa_sb[:],
+                    start=True,
+                    stop=True,
+                )
+        logits_by_token = logits[:].rearrange("p (b n) -> p b n", n=len(OTHERS))
+
+        top = held.tile([P, BLOCKS], F32, name="top")
+        nc.vector.tensor_reduce(top[:], logits_by_token, AXIS.X, ALU.max)
+        shifted = held.tile([P, BLOCKS * PROJS], F32, name="shifted")
+        shifted_by_token = shifted[:].rearrange("p (b n) -> p b n", n=PROJS)
+        nc.vector.tensor_scalar(
+            shifted_by_token[:, :, LAST : LAST + 1], top[:].unsqueeze(2), 0.0, -1.0, ALU.max, ALU.mult
+        )
+        nc.vector.tensor_tensor(
+            shifted_by_token[:, :, 0:LAST],
+            logits_by_token,
+            shifted_by_token[:, :, LAST : LAST + 1].to_broadcast([P, BLOCKS, len(OTHERS)]),
+            ALU.add,
+        )
+        grown = held.tile([P, BLOCKS * PROJS], F32, name="grown")
+        nc.scalar.activation(grown[:], shifted[:], FUNC.Exp)
+        grown_by_token = grown[:].rearrange("p (b n) -> p b n", n=PROJS)
+        total = held.tile([P, BLOCKS], F32, name="total")
+        nc.vector.tensor_reduce(total[:], grown_by_token, AXIS.X, ALU.add)
+        inverse = held.tile([P, BLOCKS], F32, name="inverse")
+        nc.vector.reciprocal(inverse[:], total[:])
+        attn = held.tile([P, BLOCKS * len(OTHERS)], F32, name="attn")
+        nc.vector.tensor_tensor(
+            attn[:].rearrange("p (b n) -> p b n", n=len(OTHERS)),
+            grown_by_token[:, :, 0:LAST],
+            inverse[:].unsqueeze(2).to_broadcast([P, BLOCKS, len(OTHERS)]),
+            ALU.mult,
+        )
+
         with tc.psum_pool(name="spread_banks", bufs=6) as spread_banks:
             for piece in range(PIECES):
-                logits = logit_banks.tile([P, BLOCKS * len(OTHERS)], F32, name="logits")
-                for n in OTHERS:
-                    for block in range(BLOCKS):
-                        column = block * len(OTHERS) + n
-                        nc.tensor.matmul(
-                            logits[:, column : column + 1],
-                            gap_bf16[piece][n][:, block * BLOCK : (block + 1) * BLOCK],
-                            wa_sb[:],
-                            start=True,
-                            stop=True,
-                        )
-                logits_by_token = logits[:].rearrange("p (b n) -> p b n", n=len(OTHERS))
-
-                top = small.tile([P, BLOCKS], F32, name="top")
-                nc.vector.tensor_reduce(top[:], logits_by_token, AXIS.X, ALU.max)
-                shifted = small.tile([P, BLOCKS * PROJS], F32, name="shifted")
-                shifted_by_token = shifted[:].rearrange("p (b n) -> p b n", n=PROJS)
-                nc.vector.tensor_scalar(
-                    shifted_by_token[:, :, LAST : LAST + 1], top[:].unsqueeze(2), 0.0, -1.0, ALU.max, ALU.mult
-                )
-                nc.vector.tensor_tensor(
-                    shifted_by_token[:, :, 0:LAST],
-                    logits_by_token,
-                    shifted_by_token[:, :, LAST : LAST + 1].to_broadcast([P, BLOCKS, len(OTHERS)]),
-                    ALU.add,
-                )
-                grown = small.tile([P, BLOCKS * PROJS], F32, name="grown")
-                nc.scalar.activation(grown[:], shifted[:], FUNC.Exp)
-                grown_by_token = grown[:].rearrange("p (b n) -> p b n", n=PROJS)
-                total = small.tile([P, BLOCKS], F32, name="total")
-                nc.vector.tensor_reduce(total[:], grown_by_token, AXIS.X, ALU.add)
-                inverse = small.tile([P, BLOCKS], F32, name="inverse")
-                nc.vector.reciprocal(inverse[:], total[:])
-                attn = small.tile([P, BLOCKS * len(OTHERS)], F32, name="attn")
-                nc.vector.tensor_tensor(
-                    attn[:].rearrange("p (b n) -> p b n", n=len(OTHERS)),
-                    grown_by_token[:, :, 0:LAST],
-                    inverse[:].unsqueeze(2).to_broadcast([P, BLOCKS, len(OTHERS)]),
-                    ALU.mult,
-                )
-
-                mixed = p_last[piece]
+                term = {}
                 for n in OTHERS:
                     spread = spread_banks.tile([P, PIECE], F32, name="spread")
-                    for block in range(BLOCKS):
-                        column = block * len(OTHERS) + n
+                    for block_in_piece in range(BLOCKS_IN_PIECE):
+                        column = (piece * BLOCKS_IN_PIECE + block_in_piece) * len(OTHERS) + n
                         nc.tensor.transpose(
-                            spread[:, block * BLOCK : (block + 1) * BLOCK],
+                            spread[:, block_in_piece * BLOCK : (block_in_piece + 1) * BLOCK],
                             attn[:, column : column + 1].to_broadcast([P, P]),
                             identity[:],
                         )
-                    term = work.tile([P, PIECE], F32, name=f"term{n}")
-                    nc.vector.tensor_tensor(term[:], spread[:], gap_f32[piece][n][:], ALU.mult)
-                    partial = work.tile([P, PIECE], F32, name=f"partial{n}")
-                    nc.vector.tensor_tensor(partial[:], mixed[:], term[:], ALU.add)
-                    mixed = partial
+                    term[n] = work.tile([P, PIECE], F32, name=f"term{n}")
+                    nc.vector.tensor_tensor(term[n][:], spread[:], gap_f32[piece][n][:], ALU.mult)
+                partial = work.tile([P, PIECE], F32, name="partial")
+                nc.gpsimd.tensor_tensor(partial[:], p_last[piece][:], term[0][:], ALU.add)
+                mixed = work.tile([P, PIECE], F32, name="mixed")
+                nc.vector.tensor_tensor(mixed[:], partial[:], term[1][:], ALU.add)
                 nc.sync.dma_start(out[:, piece * PIECE : (piece + 1) * PIECE], mixed[:])

@@ -133,7 +133,7 @@ def tile_dynamicmetaembedding_kernel(tc, table, w0, w1, w2, b0, b1, b2, wa, offs
 
         with tc.psum_pool(name="spread_banks", bufs=6) as spread_banks:
             for piece in range(PIECES):
-                term = {}
+                mixed = p_last[piece]
                 for n in OTHERS:
                     spread = spread_banks.tile([P, PIECE], F32, name="spread")
                     for block_in_piece in range(BLOCKS_IN_PIECE):
@@ -143,10 +143,9 @@ def tile_dynamicmetaembedding_kernel(tc, table, w0, w1, w2, b0, b1, b2, wa, offs
                             attn[:, column : column + 1].to_broadcast([P, P]),
                             identity[:],
                         )
-                    term[n] = work.tile([P, PIECE], F32, name=f"term{n}")
-                    nc.vector.tensor_tensor(term[n][:], spread[:], gap_f32[piece][n][:], ALU.mult)
-                partial = work.tile([P, PIECE], F32, name="partial")
-                nc.gpsimd.tensor_tensor(partial[:], p_last[piece][:], term[0][:], ALU.add)
-                mixed = work.tile([P, PIECE], F32, name="mixed")
-                nc.vector.tensor_tensor(mixed[:], partial[:], term[1][:], ALU.add)
+                    term = work.tile([P, PIECE], F32, name=f"term{n}")
+                    nc.vector.tensor_tensor(term[:], spread[:], gap_f32[piece][n][:], ALU.mult)
+                    partial = work.tile([P, PIECE], F32, name=f"partial{n}")
+                    nc.vector.tensor_tensor(partial[:], mixed[:], term[:], ALU.add)
+                    mixed = partial
                 nc.sync.dma_start(out[:, piece * PIECE : (piece + 1) * PIECE], mixed[:])

@@ -14,10 +14,10 @@ LAST = 2
 OTHERS = (0, 1)
 PIECE = 512
 BLOCK = 128
-BLOCKS = TOKENS // BLOCK
-BLOCKS_IN_PIECE = PIECE // BLOCK
+BLOCKS = PIECE // BLOCK
 PIECES = TOKENS // PIECE
 TABLE_LOADS = 4
+WARM_UP = 8
 
 FLOPS = 2 * TOKENS * PROJS * (P * P + P)
 
@@ -27,7 +27,8 @@ def tile_dynamicmetaembedding_kernel(tc, table, w0, w1, w2, b0, b1, b2, wa, offs
     with (
         tc.tile_pool(name="held", bufs=1) as held,
         tc.tile_pool(name="work", bufs=2) as work,
-        tc.psum_pool(name="logit_banks", bufs=1) as logit_banks,
+        tc.tile_pool(name="small", bufs=2) as small,
+        tc.psum_pool(name="logit_banks", bufs=2) as logit_banks,
     ):
         offsets = held.tile([P, TOKENS // 16], U16, name="offsets")
         nc.sync.dma_start(offsets[:], offs)
@@ -62,6 +63,13 @@ def tile_dynamicmetaembedding_kernel(tc, table, w0, w1, w2, b0, b1, b2, wa, offs
         one = held.tile([P, 1], F32, name="one")
         nc.scalar.activation(one[:], zero[:], FUNC.Exp)
 
+        zeros = held.tile([P, PIECE], BF16, name="zeros")
+        nc.vector.memset(zeros[:], 0.0)
+        with tc.psum_pool(name="warm_bank", bufs=1) as warm_bank:
+            unused = warm_bank.tile([P, PIECE], F32, name="unused")
+            for repeat in range(WARM_UP):
+                nc.tensor.matmul(unused[:], zeros[:, 0:P], zeros[:], start=True, stop=True)
+
         p_last, gap_f32, gap_bf16 = [], [], []
         with tc.psum_pool(name="proj_banks", bufs=6) as proj_banks:
             for piece in range(PIECES):
@@ -89,57 +97,56 @@ def tile_dynamicmetaembedding_kernel(tc, table, w0, w1, w2, b0, b1, b2, wa, offs
                 gap_f32.append(exact)
                 gap_bf16.append(rounded)
 
-        logits = logit_banks.tile([P, BLOCKS * len(OTHERS)], F32, name="logits")
-        for block in range(BLOCKS):
-            piece, block_in_piece = divmod(block, BLOCKS_IN_PIECE)
-            for n in OTHERS:
-                column = block * len(OTHERS) + n
-                nc.tensor.matmul(
-                    logits[:, column : column + 1],
-                    gap_bf16[piece][n][:, block_in_piece * BLOCK : (block_in_piece + 1) * BLOCK],
-                    wa_sb[:],
-                    start=True,
-                    stop=True,
-                )
-        logits_by_token = logits[:].rearrange("p (b n) -> p b n", n=len(OTHERS))
-
-        top = held.tile([P, BLOCKS], F32, name="top")
-        nc.vector.tensor_reduce(top[:], logits_by_token, AXIS.X, ALU.max)
-        shifted = held.tile([P, BLOCKS * PROJS], F32, name="shifted")
-        shifted_by_token = shifted[:].rearrange("p (b n) -> p b n", n=PROJS)
-        nc.vector.tensor_scalar(
-            shifted_by_token[:, :, LAST : LAST + 1], top[:].unsqueeze(2), 0.0, -1.0, ALU.max, ALU.mult
-        )
-        nc.vector.tensor_tensor(
-            shifted_by_token[:, :, 0:LAST],
-            logits_by_token,
-            shifted_by_token[:, :, LAST : LAST + 1].to_broadcast([P, BLOCKS, len(OTHERS)]),
-            ALU.add,
-        )
-        grown = held.tile([P, BLOCKS * PROJS], F32, name="grown")
-        nc.scalar.activation(grown[:], shifted[:], FUNC.Exp)
-        grown_by_token = grown[:].rearrange("p (b n) -> p b n", n=PROJS)
-        total = held.tile([P, BLOCKS], F32, name="total")
-        nc.vector.tensor_reduce(total[:], grown_by_token, AXIS.X, ALU.add)
-        inverse = held.tile([P, BLOCKS], F32, name="inverse")
-        nc.vector.reciprocal(inverse[:], total[:])
-        attn = held.tile([P, BLOCKS * len(OTHERS)], F32, name="attn")
-        nc.vector.tensor_tensor(
-            attn[:].rearrange("p (b n) -> p b n", n=len(OTHERS)),
-            grown_by_token[:, :, 0:LAST],
-            inverse[:].unsqueeze(2).to_broadcast([P, BLOCKS, len(OTHERS)]),
-            ALU.mult,
-        )
-
         with tc.psum_pool(name="spread_banks", bufs=6) as spread_banks:
             for piece in range(PIECES):
+                logits = logit_banks.tile([P, BLOCKS * len(OTHERS)], F32, name="logits")
+                for n in OTHERS:
+                    for block in range(BLOCKS):
+                        column = block * len(OTHERS) + n
+                        nc.tensor.matmul(
+                            logits[:, column : column + 1],
+                            gap_bf16[piece][n][:, block * BLOCK : (block + 1) * BLOCK],
+                            wa_sb[:],
+                            start=True,
+                            stop=True,
+                        )
+                logits_by_token = logits[:].rearrange("p (b n) -> p b n", n=len(OTHERS))
+
+                top = small.tile([P, BLOCKS], F32, name="top")
+                nc.vector.tensor_reduce(top[:], logits_by_token, AXIS.X, ALU.max)
+                shifted = small.tile([P, BLOCKS * PROJS], F32, name="shifted")
+                shifted_by_token = shifted[:].rearrange("p (b n) -> p b n", n=PROJS)
+                nc.vector.tensor_scalar(
+                    shifted_by_token[:, :, LAST : LAST + 1], top[:].unsqueeze(2), 0.0, -1.0, ALU.max, ALU.mult
+                )
+                nc.vector.tensor_tensor(
+                    shifted_by_token[:, :, 0:LAST],
+                    logits_by_token,
+                    shifted_by_token[:, :, LAST : LAST + 1].to_broadcast([P, BLOCKS, len(OTHERS)]),
+                    ALU.add,
+                )
+                grown = small.tile([P, BLOCKS * PROJS], F32, name="grown")
+                nc.scalar.activation(grown[:], shifted[:], FUNC.Exp)
+                grown_by_token = grown[:].rearrange("p (b n) -> p b n", n=PROJS)
+                total = small.tile([P, BLOCKS], F32, name="total")
+                nc.vector.tensor_reduce(total[:], grown_by_token, AXIS.X, ALU.add)
+                inverse = small.tile([P, BLOCKS], F32, name="inverse")
+                nc.vector.reciprocal(inverse[:], total[:])
+                attn = small.tile([P, BLOCKS * len(OTHERS)], F32, name="attn")
+                nc.vector.tensor_tensor(
+                    attn[:].rearrange("p (b n) -> p b n", n=len(OTHERS)),
+                    grown_by_token[:, :, 0:LAST],
+                    inverse[:].unsqueeze(2).to_broadcast([P, BLOCKS, len(OTHERS)]),
+                    ALU.mult,
+                )
+
                 mixed = p_last[piece]
                 for n in OTHERS:
                     spread = spread_banks.tile([P, PIECE], F32, name="spread")
-                    for block_in_piece in range(BLOCKS_IN_PIECE):
-                        column = (piece * BLOCKS_IN_PIECE + block_in_piece) * len(OTHERS) + n
+                    for block in range(BLOCKS):
+                        column = block * len(OTHERS) + n
                         nc.tensor.transpose(
-                            spread[:, block_in_piece * BLOCK : (block_in_piece + 1) * BLOCK],
+                            spread[:, block * BLOCK : (block + 1) * BLOCK],
                             attn[:, column : column + 1].to_broadcast([P, P]),
                             identity[:],
                         )

@@ -17,7 +17,6 @@ BLOCK = 128
 BLOCKS = PIECE // BLOCK
 PIECES = TOKENS // PIECE
 TABLE_LOADS = 4
-WARM_UP = 8
 
 FLOPS = 2 * TOKENS * PROJS * (P * P + P)
 
@@ -63,13 +62,6 @@ def tile_dynamicmetaembedding_kernel(tc, table, w0, w1, w2, b0, b1, b2, wa, offs
         one = held.tile([P, 1], F32, name="one")
         nc.scalar.activation(one[:], zero[:], FUNC.Exp)
 
-        zeros = held.tile([P, PIECE], BF16, name="zeros")
-        nc.vector.memset(zeros[:], 0.0)
-        with tc.psum_pool(name="warm_bank", bufs=1) as warm_bank:
-            unused = warm_bank.tile([P, PIECE], F32, name="unused")
-            for repeat in range(WARM_UP):
-                nc.tensor.matmul(unused[:], zeros[:, 0:P], zeros[:], start=True, stop=True)
-
         p_last, gap_f32, gap_bf16 = [], [], []
         with tc.psum_pool(name="proj_banks", bufs=6) as proj_banks:
             for piece in range(PIECES):
@@ -97,7 +89,10 @@ def tile_dynamicmetaembedding_kernel(tc, table, w0, w1, w2, b0, b1, b2, wa, offs
                 gap_f32.append(exact)
                 gap_bf16.append(rounded)
 
-        with tc.psum_pool(name="spread_banks", bufs=6) as spread_banks:
+        with (
+            tc.psum_pool(name="flipped_banks", bufs=4) as flipped_banks,
+            tc.psum_pool(name="back_banks", bufs=2) as back_banks,
+        ):
             for piece in range(PIECES):
                 logits = logit_banks.tile([P, BLOCKS * len(OTHERS)], F32, name="logits")
                 for n in OTHERS:
@@ -140,19 +135,23 @@ def tile_dynamicmetaembedding_kernel(tc, table, w0, w1, w2, b0, b1, b2, wa, offs
                     ALU.mult,
                 )
 
-                mixed = p_last[piece]
+                flipped = {}
                 for n in OTHERS:
-                    spread = spread_banks.tile([P, PIECE], F32, name="spread")
+                    flipped[n] = flipped_banks.tile([P, PIECE], F32, name="flipped")
                     for block in range(BLOCKS):
-                        column = block * len(OTHERS) + n
-                        nc.tensor.transpose(
-                            spread[:, block * BLOCK : (block + 1) * BLOCK],
-                            attn[:, column : column + 1].to_broadcast([P, P]),
-                            identity[:],
-                        )
-                    term = work.tile([P, PIECE], F32, name=f"term{n}")
-                    nc.vector.tensor_tensor(term[:], spread[:], gap_f32[piece][n][:], ALU.mult)
-                    partial = work.tile([P, PIECE], F32, name=f"partial{n}")
-                    nc.vector.tensor_tensor(partial[:], mixed[:], term[:], ALU.add)
-                    mixed = partial
+                        columns = slice(block * BLOCK, (block + 1) * BLOCK)
+                        nc.tensor.transpose(flipped[n][:, columns], gap_f32[piece][n][:, columns], identity[:])
+                first = work.tile([P, PIECE], F32, name="first")
+                both = work.tile([P, PIECE], F32, name="both")
+                back = back_banks.tile([P, PIECE], F32, name="back")
+                for block in range(BLOCKS):
+                    columns = slice(block * BLOCK, (block + 1) * BLOCK)
+                    weight = [attn[:, block * len(OTHERS) + n : block * len(OTHERS) + n + 1] for n in OTHERS]
+                    nc.scalar.activation(first[:, columns], flipped[0][:, columns], FUNC.Copy, scale=weight[0])
+                    nc.vector.scalar_tensor_tensor(
+                        both[:, columns], flipped[1][:, columns], weight[1], first[:, columns], ALU.mult, ALU.add
+                    )
+                    nc.tensor.transpose(back[:, columns], both[:, columns], identity[:])
+                mixed = work.tile([P, PIECE], F32, name="mixed")
+                nc.vector.tensor_tensor(mixed[:], back[:], p_last[piece][:], ALU.add)
                 nc.sync.dma_start(out[:, piece * PIECE : (piece + 1) * PIECE], mixed[:])

@@ -16,6 +16,7 @@ PIECE = 512
 BLOCK = 128
 BLOCKS = PIECE // BLOCK
 PIECES = TOKENS // PIECE
+PAIR = 2
 TABLE_LOADS = 4
 
 FLOPS = 2 * TOKENS * PROJS * (P * P + P)
@@ -93,23 +94,24 @@ def tile_dynamicmetaembedding_kernel(tc, table, w0, w1, w2, b0, b1, b2, wa, offs
             tc.psum_pool(name="flipped_banks", bufs=4) as flipped_banks,
             tc.psum_pool(name="back_banks", bufs=2) as back_banks,
         ):
-            for piece in range(PIECES):
-                logits = logit_banks.tile([P, BLOCKS * len(OTHERS)], F32, name="logits")
-                for n in OTHERS:
-                    for block in range(BLOCKS):
+            for pair in range(PIECES // PAIR):
+                logits = logit_banks.tile([P, PAIR * BLOCKS * len(OTHERS)], F32, name="logits")
+                for block in range(PAIR * BLOCKS):
+                    piece, block_in_piece = pair * PAIR + block // BLOCKS, block % BLOCKS
+                    for n in OTHERS:
                         column = block * len(OTHERS) + n
                         nc.tensor.matmul(
                             logits[:, column : column + 1],
-                            gap_bf16[piece][n][:, block * BLOCK : (block + 1) * BLOCK],
+                            gap_bf16[piece][n][:, block_in_piece * BLOCK : (block_in_piece + 1) * BLOCK],
                             wa_sb[:],
                             start=True,
                             stop=True,
                         )
                 logits_by_token = logits[:].rearrange("p (b n) -> p b n", n=len(OTHERS))
 
-                top = small.tile([P, BLOCKS], F32, name="top")
+                top = small.tile([P, PAIR * BLOCKS], F32, name="top")
                 nc.vector.tensor_reduce(top[:], logits_by_token, AXIS.X, ALU.max)
-                shifted = small.tile([P, BLOCKS * PROJS], F32, name="shifted")
+                shifted = small.tile([P, PAIR * BLOCKS * PROJS], F32, name="shifted")
                 shifted_by_token = shifted[:].rearrange("p (b n) -> p b n", n=PROJS)
                 nc.vector.tensor_scalar(
                     shifted_by_token[:, :, LAST : LAST + 1], top[:].unsqueeze(2), 0.0, -1.0, ALU.max, ALU.mult
@@ -117,41 +119,43 @@ def tile_dynamicmetaembedding_kernel(tc, table, w0, w1, w2, b0, b1, b2, wa, offs
                 nc.vector.tensor_tensor(
                     shifted_by_token[:, :, 0:LAST],
                     logits_by_token,
-                    shifted_by_token[:, :, LAST : LAST + 1].to_broadcast([P, BLOCKS, len(OTHERS)]),
+                    shifted_by_token[:, :, LAST : LAST + 1].to_broadcast([P, PAIR * BLOCKS, len(OTHERS)]),
                     ALU.add,
                 )
-                grown = small.tile([P, BLOCKS * PROJS], F32, name="grown")
+                grown = small.tile([P, PAIR * BLOCKS * PROJS], F32, name="grown")
                 nc.scalar.activation(grown[:], shifted[:], FUNC.Exp)
                 grown_by_token = grown[:].rearrange("p (b n) -> p b n", n=PROJS)
-                total = small.tile([P, BLOCKS], F32, name="total")
+                total = small.tile([P, PAIR * BLOCKS], F32, name="total")
                 nc.vector.tensor_reduce(total[:], grown_by_token, AXIS.X, ALU.add)
-                inverse = small.tile([P, BLOCKS], F32, name="inverse")
+                inverse = small.tile([P, PAIR * BLOCKS], F32, name="inverse")
                 nc.vector.reciprocal(inverse[:], total[:])
-                attn = small.tile([P, BLOCKS * len(OTHERS)], F32, name="attn")
+                attn = small.tile([P, PAIR * BLOCKS * len(OTHERS)], F32, name="attn")
                 nc.vector.tensor_tensor(
                     attn[:].rearrange("p (b n) -> p b n", n=len(OTHERS)),
                     grown_by_token[:, :, 0:LAST],
-                    inverse[:].unsqueeze(2).to_broadcast([P, BLOCKS, len(OTHERS)]),
+                    inverse[:].unsqueeze(2).to_broadcast([P, PAIR * BLOCKS, len(OTHERS)]),
                     ALU.mult,
                 )
 
-                flipped = {}
-                for n in OTHERS:
-                    flipped[n] = flipped_banks.tile([P, PIECE], F32, name="flipped")
+                for piece in range(pair * PAIR, (pair + 1) * PAIR):
+                    flipped = {}
+                    for n in OTHERS:
+                        flipped[n] = flipped_banks.tile([P, PIECE], F32, name="flipped")
+                        for block in range(BLOCKS):
+                            columns = slice(block * BLOCK, (block + 1) * BLOCK)
+                            nc.tensor.transpose(flipped[n][:, columns], gap_f32[piece][n][:, columns], identity[:])
+                    first = work.tile([P, PIECE], F32, name="first")
+                    both = work.tile([P, PIECE], F32, name="both")
+                    back = back_banks.tile([P, PIECE], F32, name="back")
                     for block in range(BLOCKS):
                         columns = slice(block * BLOCK, (block + 1) * BLOCK)
-                        nc.tensor.transpose(flipped[n][:, columns], gap_f32[piece][n][:, columns], identity[:])
-                first = work.tile([P, PIECE], F32, name="first")
-                both = work.tile([P, PIECE], F32, name="both")
-                back = back_banks.tile([P, PIECE], F32, name="back")
-                for block in range(BLOCKS):
-                    columns = slice(block * BLOCK, (block + 1) * BLOCK)
-                    weight = [attn[:, block * len(OTHERS) + n : block * len(OTHERS) + n + 1] for n in OTHERS]
-                    nc.scalar.activation(first[:, columns], flipped[0][:, columns], FUNC.Copy, scale=weight[0])
-                    nc.vector.scalar_tensor_tensor(
-                        both[:, columns], flipped[1][:, columns], weight[1], first[:, columns], ALU.mult, ALU.add
-                    )
-                    nc.tensor.transpose(back[:, columns], both[:, columns], identity[:])
-                mixed = work.tile([P, PIECE], F32, name="mixed")
-                nc.vector.tensor_tensor(mixed[:], back[:], p_last[piece][:], ALU.add)
-                nc.sync.dma_start(out[:, piece * PIECE : (piece + 1) * PIECE], mixed[:])
+                        first_column = ((piece % PAIR) * BLOCKS + block) * len(OTHERS)
+                        weight = [attn[:, first_column + n : first_column + n + 1] for n in OTHERS]
+                        nc.scalar.activation(first[:, columns], flipped[0][:, columns], FUNC.Copy, scale=weight[0])
+                        nc.vector.scalar_tensor_tensor(
+                            both[:, columns], flipped[1][:, columns], weight[1], first[:, columns], ALU.mult, ALU.add
+                        )
+                        nc.tensor.transpose(back[:, columns], both[:, columns], identity[:])
+                    mixed = work.tile([P, PIECE], F32, name="mixed")
+                    nc.vector.tensor_tensor(mixed[:], back[:], p_last[piece][:], ALU.add)
+                    nc.sync.dma_start(out[:, piece * PIECE : (piece + 1) * PIECE], mixed[:])

@@ -17,7 +17,7 @@ BLOCK = 128
 BLOCKS = PIECE // BLOCK
 PIECES = TOKENS // PIECE
 PAIR = 2
-TABLE_LOADS = 4
+TABLE_LOADS = 2
 
 FLOPS = 2 * TOKENS * PROJS * (P * P + P)
 
@@ -30,30 +30,25 @@ def tile_dynamicmetaembedding_kernel(tc, table, w0, w1, w2, b0, b1, b2, wa, offs
         tc.tile_pool(name="small", bufs=2) as small,
         tc.psum_pool(name="logit_banks", bufs=2) as logit_banks,
     ):
-        offsets = held.tile([P, TOKENS // 16], U16, name="offsets")
-        nc.sync.dma_start(offsets[:], offs)
-
-        w_sb = []
-        for n, w in enumerate((w0, w1, w2)):
-            w_tile = held.tile([P, P], BF16, name=f"w{n}_sb")
-            nc.scalar.dma_start(w_tile[:], w)
-            w_sb.append(w_tile)
-
         table_sb = held.tile([P, WORDS], BF16, name="table_sb")
         span = WORDS // TABLE_LOADS
-        for part in range(TABLE_LOADS):
-            queue = nc.sync if part % 2 == 0 else nc.scalar
+        for part, queue in enumerate((nc.sync, nc.scalar)):
             queue.dma_start(
                 table_sb[:, part * span : (part + 1) * span], table[:, part * span : (part + 1) * span]
             )
+        offsets = held.tile([P, TOKENS // 16], U16, name="offsets")
+        nc.sync.dma_start(offsets[:], offs)
 
-        b_sb = []
-        for n, b in enumerate((b0, b1, b2)):
-            b_tile = held.tile([P, 1], F32, name=f"b{n}_sb")
-            nc.sync.dma_start(b_tile[:], b)
-            b_sb.append(b_tile)
+        w_sb = [held.tile([P, P], BF16, name=f"w{n}_sb") for n in range(PROJS)]
+        b_sb = [held.tile([P, 1], F32, name=f"b{n}_sb") for n in range(PROJS)]
         wa_sb = held.tile([P, 1], BF16, name="wa_sb")
-        nc.scalar.dma_start(wa_sb[:], wa)
+        nc.scalar.dma_start(w_sb[LAST][:], w2)
+        nc.scalar.dma_start(b_sb[LAST][:], b2)
+        nc.sync.dma_start(w_sb[0][:], w0)
+        nc.sync.dma_start(w_sb[1][:], w1)
+        nc.sync.dma_start(b_sb[0][:], b0)
+        nc.sync.dma_start(b_sb[1][:], b1)
+        nc.sync.dma_start(wa_sb[:], wa)
 
         identity = held.tile([P, P], F32, name="identity")
         make_identity(nc, identity[:])
@@ -85,8 +80,8 @@ def tile_dynamicmetaembedding_kernel(tc, table, w0, w1, w2, b0, b1, b2, wa, offs
                         exact[n][:], proj[n][:], b_sb[n][:], last[:], ALU.add, ALU.subtract
                     )
                     rounded[n] = held.tile([P, PIECE], BF16, name=f"gap{n}_bf16_{piece}")
-                nc.scalar.activation(rounded[0][:], exact[0][:], FUNC.Copy)
-                nc.vector.tensor_copy(rounded[1][:], exact[1][:])
+                nc.gpsimd.tensor_copy(rounded[0][:], exact[0][:])
+                nc.scalar.activation(rounded[1][:], exact[1][:], FUNC.Copy)
                 gap_f32.append(exact)
                 gap_bf16.append(rounded)
 

@@ -4,7 +4,6 @@ from concourse.masks import make_identity
 BF16, F32, U16 = mybir.dt.bfloat16, mybir.dt.float32, mybir.dt.uint16
 FUNC = mybir.ActivationFunctionType
 ALU = mybir.AluOpType
-AXIS = mybir.AxisListType
 
 P = 128
 WORDS = 4096
@@ -18,6 +17,9 @@ BLOCKS = PIECE // BLOCK
 PIECES = TOKENS // PIECE
 PAIR = 2
 TABLE_LOADS = 2
+SIGNS = ((-1.0, -1.0, 1.0, 0.0), (0.0, 1.0, -1.0, -1.0))
+EXPONENTS = 4
+TERMS = EXPONENTS // len(OTHERS)
 
 FLOPS = 2 * TOKENS * PROJS * (P * P + P)
 
@@ -58,6 +60,13 @@ def tile_dynamicmetaembedding_kernel(tc, table, w0, w1, w2, b0, b1, b2, wa, offs
         one = held.tile([P, 1], F32, name="one")
         nc.scalar.activation(one[:], zero[:], FUNC.Exp)
 
+        signs = held.tile([P, len(OTHERS) * EXPONENTS], F32, name="signs")
+        for n in OTHERS:
+            for e, sign in enumerate(SIGNS[n]):
+                nc.gpsimd.memset(signs[:, n * EXPONENTS + e : n * EXPONENTS + e + 1], sign)
+        signed_wa = held.tile([P, len(OTHERS) * EXPONENTS], BF16, name="signed_wa")
+        nc.gpsimd.tensor_scalar_mul(signed_wa[:], signs[:], wa_sb[:])
+
         p_last, gap_f32, gap_bf16 = [], [], []
         with tc.psum_pool(name="proj_banks", bufs=6) as proj_banks:
             for piece in range(PIECES):
@@ -90,47 +99,27 @@ def tile_dynamicmetaembedding_kernel(tc, table, w0, w1, w2, b0, b1, b2, wa, offs
             tc.psum_pool(name="back_banks", bufs=2) as back_banks,
         ):
             for pair in range(PIECES // PAIR):
-                logits = logit_banks.tile([P, PAIR * BLOCKS * len(OTHERS)], F32, name="logits")
+                exponents = logit_banks.tile([P, PAIR * BLOCKS * EXPONENTS], F32, name="exponents")
                 for block in range(PAIR * BLOCKS):
                     piece, block_in_piece = pair * PAIR + block // BLOCKS, block % BLOCKS
                     for n in OTHERS:
-                        column = block * len(OTHERS) + n
                         nc.tensor.matmul(
-                            logits[:, column : column + 1],
+                            exponents[:, block * EXPONENTS : (block + 1) * EXPONENTS],
                             gap_bf16[piece][n][:, block_in_piece * BLOCK : (block_in_piece + 1) * BLOCK],
-                            wa_sb[:],
-                            start=True,
-                            stop=True,
+                            signed_wa[:, n * EXPONENTS : (n + 1) * EXPONENTS],
+                            start=(n == OTHERS[0]),
+                            stop=(n == OTHERS[-1]),
                         )
-                logits_by_token = logits[:].rearrange("p (b n) -> p b n", n=len(OTHERS))
 
-                top = small.tile([P, PAIR * BLOCKS], F32, name="top")
-                nc.vector.tensor_reduce(top[:], logits_by_token, AXIS.X, ALU.max)
-                shifted = small.tile([P, PAIR * BLOCKS * PROJS], F32, name="shifted")
-                shifted_by_token = shifted[:].rearrange("p (b n) -> p b n", n=PROJS)
-                nc.vector.tensor_scalar(
-                    shifted_by_token[:, :, LAST : LAST + 1], top[:].unsqueeze(2), 0.0, -1.0, ALU.max, ALU.mult
+                grown = small.tile([P, PAIR * BLOCKS * EXPONENTS], F32, name="grown")
+                nc.scalar.activation(grown[:], exponents[:], FUNC.Exp)
+                grown_by_weight = grown[:].rearrange("p (w t) -> p w t", t=TERMS)
+                total = small.tile([P, PAIR * BLOCKS * len(OTHERS)], F32, name="total")
+                nc.vector.scalar_tensor_tensor(
+                    total[:].unsqueeze(2), grown_by_weight[:, :, 0:1], 1.0, grown_by_weight[:, :, 1:2], ALU.add, ALU.add
                 )
-                nc.vector.tensor_tensor(
-                    shifted_by_token[:, :, 0:LAST],
-                    logits_by_token,
-                    shifted_by_token[:, :, LAST : LAST + 1].to_broadcast([P, PAIR * BLOCKS, len(OTHERS)]),
-                    ALU.add,
-                )
-                grown = small.tile([P, PAIR * BLOCKS * PROJS], F32, name="grown")
-                nc.scalar.activation(grown[:], shifted[:], FUNC.Exp)
-                grown_by_token = grown[:].rearrange("p (b n) -> p b n", n=PROJS)
-                total = small.tile([P, PAIR * BLOCKS], F32, name="total")
-                nc.vector.tensor_reduce(total[:], grown_by_token, AXIS.X, ALU.add)
-                inverse = small.tile([P, PAIR * BLOCKS], F32, name="inverse")
-                nc.vector.reciprocal(inverse[:], total[:])
                 attn = small.tile([P, PAIR * BLOCKS * len(OTHERS)], F32, name="attn")
-                nc.vector.tensor_tensor(
-                    attn[:].rearrange("p (b n) -> p b n", n=len(OTHERS)),
-                    grown_by_token[:, :, 0:LAST],
-                    inverse[:].unsqueeze(2).to_broadcast([P, PAIR * BLOCKS, len(OTHERS)]),
-                    ALU.mult,
-                )
+                nc.vector.reciprocal(attn[:], total[:])
 
                 for piece in range(pair * PAIR, (pair + 1) * PAIR):
                     flipped = {}

@@ -46,11 +46,11 @@ def tile_dynamicmetaembedding_kernel(tc, table, w0, w1, w2, b0, b1, b2, wa, offs
         wa_sb = held.tile([P, 1], BF16, name="wa_sb")
         nc.scalar.dma_start(w_sb[LAST][:], w2)
         nc.scalar.dma_start(b_sb[LAST][:], b2)
+        nc.sync.dma_start(wa_sb[:], wa)
         nc.sync.dma_start(w_sb[0][:], w0)
         nc.sync.dma_start(w_sb[1][:], w1)
         nc.sync.dma_start(b_sb[0][:], b0)
         nc.sync.dma_start(b_sb[1][:], b1)
-        nc.sync.dma_start(wa_sb[:], wa)
 
         identity = held.tile([P, P], F32, name="identity")
         make_identity(nc, identity[:])
@@ -63,9 +63,9 @@ def tile_dynamicmetaembedding_kernel(tc, table, w0, w1, w2, b0, b1, b2, wa, offs
         signs = held.tile([P, len(OTHERS) * EXPONENTS], F32, name="signs")
         for n in OTHERS:
             for e, sign in enumerate(SIGNS[n]):
-                nc.gpsimd.memset(signs[:, n * EXPONENTS + e : n * EXPONENTS + e + 1], sign)
+                nc.vector.memset(signs[:, n * EXPONENTS + e : n * EXPONENTS + e + 1], sign)
         signed_wa = held.tile([P, len(OTHERS) * EXPONENTS], BF16, name="signed_wa")
-        nc.gpsimd.tensor_scalar_mul(signed_wa[:], signs[:], wa_sb[:])
+        nc.vector.tensor_scalar_mul(signed_wa[:], signs[:], wa_sb[:])
 
         p_last, gap_f32, gap_bf16 = [], [], []
         with tc.psum_pool(name="proj_banks", bufs=6) as proj_banks:

@@ -30,7 +30,8 @@ def tile_dynamicmetaembedding_kernel(tc, table, w0, w1, w2, b0, b1, b2, wa, offs
         tc.tile_pool(name="held", bufs=1) as held,
         tc.tile_pool(name="work", bufs=2) as work,
         tc.tile_pool(name="small", bufs=2) as small,
-        tc.psum_pool(name="logit_banks", bufs=2) as logit_banks,
+        tc.psum_pool(name="shared_banks", bufs=6) as shared_banks,
+        tc.psum_pool(name="back_banks", bufs=2) as back_banks,
     ):
         table_sb = held.tile([P, WORDS], BF16, name="table_sb")
         span = WORDS // TABLE_LOADS
@@ -68,78 +69,73 @@ def tile_dynamicmetaembedding_kernel(tc, table, w0, w1, w2, b0, b1, b2, wa, offs
         nc.vector.tensor_scalar_mul(signed_wa[:], signs[:], wa_sb[:])
 
         p_last, gap_f32, gap_bf16 = [], [], []
-        with tc.psum_pool(name="proj_banks", bufs=6) as proj_banks:
-            for piece in range(PIECES):
-                piece_offsets = offsets[:, piece * (PIECE // 16) : (piece + 1) * (PIECE // 16)]
-                proj = {}
-                for n in (LAST,) + OTHERS:
-                    proj[n] = proj_banks.tile([P, PIECE], F32, name="proj")
-                    nc.tensor.matmul(
-                        proj[n][:], w_sb[n][:], table_sb[:].indirect(piece_offsets), start=True, stop=True
-                    )
-
-                last = held.tile([P, PIECE], F32, name=f"p_last_{piece}")
-                nc.scalar.activation(last[:], proj[LAST][:], FUNC.Identity, bias=b_sb[LAST][:])
-                p_last.append(last)
-
-                exact, rounded = {}, {}
-                for n in OTHERS:
-                    exact[n] = held.tile([P, PIECE], F32, name=f"gap{n}_f32_{piece}")
-                    nc.vector.scalar_tensor_tensor(
-                        exact[n][:], proj[n][:], b_sb[n][:], last[:], ALU.add, ALU.subtract
-                    )
-                    rounded[n] = held.tile([P, PIECE], BF16, name=f"gap{n}_bf16_{piece}")
-                nc.gpsimd.tensor_copy(rounded[0][:], exact[0][:])
-                nc.scalar.activation(rounded[1][:], exact[1][:], FUNC.Copy)
-                gap_f32.append(exact)
-                gap_bf16.append(rounded)
-
-        with (
-            tc.psum_pool(name="flipped_banks", bufs=4) as flipped_banks,
-            tc.psum_pool(name="back_banks", bufs=2) as back_banks,
-        ):
-            for pair in range(PIECES // PAIR):
-                exponents = logit_banks.tile([P, PAIR * BLOCKS * EXPONENTS], F32, name="exponents")
-                for block in range(PAIR * BLOCKS):
-                    piece, block_in_piece = pair * PAIR + block // BLOCKS, block % BLOCKS
-                    for n in OTHERS:
-                        nc.tensor.matmul(
-                            exponents[:, block * EXPONENTS : (block + 1) * EXPONENTS],
-                            gap_bf16[piece][n][:, block_in_piece * BLOCK : (block_in_piece + 1) * BLOCK],
-                            signed_wa[:, n * EXPONENTS : (n + 1) * EXPONENTS],
-                            start=(n == OTHERS[0]),
-                            stop=(n == OTHERS[-1]),
-                        )
-
-                grown = small.tile([P, PAIR * BLOCKS * EXPONENTS], F32, name="grown")
-                nc.scalar.activation(grown[:], exponents[:], FUNC.Exp)
-                grown_by_weight = grown[:].rearrange("p (w t) -> p w t", t=TERMS)
-                total = small.tile([P, PAIR * BLOCKS * len(OTHERS)], F32, name="total")
-                nc.vector.scalar_tensor_tensor(
-                    total[:].unsqueeze(2), grown_by_weight[:, :, 0:1], 1.0, grown_by_weight[:, :, 1:2], ALU.add, ALU.add
+        for piece in range(PIECES):
+            piece_offsets = offsets[:, piece * (PIECE // 16) : (piece + 1) * (PIECE // 16)]
+            proj = {}
+            for n in (LAST,) + OTHERS:
+                proj[n] = shared_banks.tile([P, PIECE], F32, name="proj", tag="bank")
+                nc.tensor.matmul(
+                    proj[n][:], w_sb[n][:], table_sb[:].indirect(piece_offsets), start=True, stop=True
                 )
-                attn = small.tile([P, PAIR * BLOCKS * len(OTHERS)], F32, name="attn")
-                nc.vector.reciprocal(attn[:], total[:])
 
-                for piece in range(pair * PAIR, (pair + 1) * PAIR):
-                    flipped = {}
-                    for n in OTHERS:
-                        flipped[n] = flipped_banks.tile([P, PIECE], F32, name="flipped")
-                        for block in range(BLOCKS):
-                            columns = slice(block * BLOCK, (block + 1) * BLOCK)
-                            nc.tensor.transpose(flipped[n][:, columns], gap_f32[piece][n][:, columns], identity[:])
-                    first = work.tile([P, PIECE], F32, name="first")
-                    both = work.tile([P, PIECE], F32, name="both")
-                    back = back_banks.tile([P, PIECE], F32, name="back")
+            last = held.tile([P, PIECE], F32, name=f"p_last_{piece}")
+            nc.scalar.activation(last[:], proj[LAST][:], FUNC.Identity, bias=b_sb[LAST][:])
+            p_last.append(last)
+
+            exact, rounded = {}, {}
+            for n in OTHERS:
+                exact[n] = held.tile([P, PIECE], F32, name=f"gap{n}_f32_{piece}")
+                nc.vector.scalar_tensor_tensor(
+                    exact[n][:], proj[n][:], b_sb[n][:], last[:], ALU.add, ALU.subtract
+                )
+                rounded[n] = held.tile([P, PIECE], BF16, name=f"gap{n}_bf16_{piece}")
+            nc.scalar.activation(rounded[0][:], exact[0][:], FUNC.Copy)
+            nc.vector.tensor_copy(rounded[1][:], exact[1][:])
+            gap_f32.append(exact)
+            gap_bf16.append(rounded)
+
+        for pair in range(PIECES // PAIR):
+            exponents = shared_banks.tile([P, PAIR * BLOCKS * EXPONENTS], F32, name="exponents", tag="bank")
+            for block in range(PAIR * BLOCKS):
+                piece, block_in_piece = pair * PAIR + block // BLOCKS, block % BLOCKS
+                for n in OTHERS:
+                    nc.tensor.matmul(
+                        exponents[:, block * EXPONENTS : (block + 1) * EXPONENTS],
+                        gap_bf16[piece][n][:, block_in_piece * BLOCK : (block_in_piece + 1) * BLOCK],
+                        signed_wa[:, n * EXPONENTS : (n + 1) * EXPONENTS],
+                        start=(n == OTHERS[0]),
+                        stop=(n == OTHERS[-1]),
+                    )
+
+            grown = small.tile([P, PAIR * BLOCKS * EXPONENTS], F32, name="grown")
+            nc.scalar.activation(grown[:], exponents[:], FUNC.Exp)
+            grown_by_weight = grown[:].rearrange("p (w t) -> p w t", t=TERMS)
+            total = small.tile([P, PAIR * BLOCKS * len(OTHERS)], F32, name="total")
+            nc.vector.scalar_tensor_tensor(
+                total[:].unsqueeze(2), grown_by_weight[:, :, 0:1], 1.0, grown_by_weight[:, :, 1:2], ALU.add, ALU.add
+            )
+            attn = small.tile([P, PAIR * BLOCKS * len(OTHERS)], F32, name="attn")
+            nc.vector.reciprocal(attn[:], total[:])
+
+            for piece in range(pair * PAIR, (pair + 1) * PAIR):
+                flipped = {}
+                for n in OTHERS:
+                    flipped[n] = shared_banks.tile([P, PIECE], F32, name="flipped", tag="bank")
                     for block in range(BLOCKS):
                         columns = slice(block * BLOCK, (block + 1) * BLOCK)
-                        first_column = ((piece % PAIR) * BLOCKS + block) * len(OTHERS)
-                        weight = [attn[:, first_column + n : first_column + n + 1] for n in OTHERS]
-                        nc.scalar.activation(first[:, columns], flipped[0][:, columns], FUNC.Copy, scale=weight[0])
-                        nc.vector.scalar_tensor_tensor(
-                            both[:, columns], flipped[1][:, columns], weight[1], first[:, columns], ALU.mult, ALU.add
-                        )
-                        nc.tensor.transpose(back[:, columns], both[:, columns], identity[:])
-                    mixed = work.tile([P, PIECE], F32, name="mixed")
-                    nc.vector.tensor_tensor(mixed[:], back[:], p_last[piece][:], ALU.add)
-                    nc.sync.dma_start(out[:, piece * PIECE : (piece + 1) * PIECE], mixed[:])
+                        nc.tensor.transpose(flipped[n][:, columns], gap_f32[piece][n][:, columns], identity[:])
+                first = work.tile([P, PIECE], F32, name="first")
+                both = work.tile([P, PIECE], F32, name="both")
+                back = back_banks.tile([P, PIECE], F32, name="back")
+                for block in range(BLOCKS):
+                    columns = slice(block * BLOCK, (block + 1) * BLOCK)
+                    first_column = ((piece % PAIR) * BLOCKS + block) * len(OTHERS)
+                    weight = [attn[:, first_column + n : first_column + n + 1] for n in OTHERS]
+                    nc.scalar.activation(first[:, columns], flipped[0][:, columns], FUNC.Copy, scale=weight[0])
+                    nc.vector.scalar_tensor_tensor(
+                        both[:, columns], flipped[1][:, columns], weight[1], first[:, columns], ALU.mult, ALU.add
+                    )
+                    nc.tensor.transpose(back[:, columns], both[:, columns], identity[:])
+                mixed = work.tile([P, PIECE], F32, name="mixed")
+                nc.vector.tensor_tensor(mixed[:], back[:], p_last[piece][:], ALU.add)
+                nc.sync.dma_start(out[:, piece * PIECE : (piece + 1) * PIECE], mixed[:])

@@ -126,7 +126,11 @@ def tile_dynamicmetaembedding_kernel(tc, table, w0, w1, w2, b0, b1, b2, wa, offs
                         nc.tensor.transpose(flipped[n][:, columns], gap_f32[piece][n][:, columns], identity[:])
                 first = work.tile([P, PIECE], F32, name="first")
                 both = work.tile([P, PIECE], F32, name="both")
-                back = back_banks.tile([P, PIECE], F32, name="back")
+                parts = 2 if piece == PIECES - 1 else 1
+                width = PIECE // parts
+                backs = [back_banks.tile([P, width], F32, name="back")]
+                if parts == 2:
+                    backs.append(shared_banks.tile([P, width], F32, name="back_end", tag="bank"))
                 for block in range(BLOCKS):
                     columns = slice(block * BLOCK, (block + 1) * BLOCK)
                     first_column = ((piece % PAIR) * BLOCKS + block) * len(OTHERS)
@@ -135,7 +139,20 @@ def tile_dynamicmetaembedding_kernel(tc, table, w0, w1, w2, b0, b1, b2, wa, offs
                     nc.vector.scalar_tensor_tensor(
                         both[:, columns], flipped[1][:, columns], weight[1], first[:, columns], ALU.mult, ALU.add
                     )
-                    nc.tensor.transpose(back[:, columns], both[:, columns], identity[:])
-                mixed = work.tile([P, PIECE], F32, name="mixed")
-                nc.vector.tensor_tensor(mixed[:], back[:], p_last[piece][:], ALU.add)
-                nc.sync.dma_start(out[:, piece * PIECE : (piece + 1) * PIECE], mixed[:])
+                    back, column = backs[block * BLOCK // width], block * BLOCK % width
+                    nc.tensor.transpose(back[:, column : column + BLOCK], both[:, columns], identity[:])
+                mixed = held.tile([P, PIECE], F32, name=f"mixed_{piece}")
+                if piece == 0:
+                    copied = work.tile([P, PIECE], F32, name="copied")
+                    nc.scalar.activation(copied[:], backs[0][:], FUNC.Copy)
+                    nc.gpsimd.tensor_tensor(mixed[:], copied[:], p_last[piece][:], ALU.add)
+                else:
+                    for part, back in enumerate(backs):
+                        columns = slice(part * width, (part + 1) * width)
+                        nc.vector.tensor_tensor(mixed[:, columns], back[:], p_last[piece][:, columns], ALU.add)
+                for part in range(parts):
+                    queue = (nc.sync, nc.scalar)[part]
+                    columns = slice(part * width, (part + 1) * width)
+                    queue.dma_start(
+                        out[:, piece * PIECE + part * width : piece * PIECE + (part + 1) * width], mixed[:, columns]
+                    )

@@ -117,13 +117,18 @@ def tile_dynamicmetaembedding_kernel(tc, table, w0, w1, w2, b0, b1, b2, wa, offs
             attn = small.tile([P, PAIR * BLOCKS * len(OTHERS)], F32, name="attn")
             nc.vector.reciprocal(attn[:], total[:])
 
+            flipped_pair = {}
             for piece in range(pair * PAIR, (pair + 1) * PAIR):
-                flipped = {}
+                flipped_pair[piece] = {}
                 for n in OTHERS:
-                    flipped[n] = shared_banks.tile([P, PIECE], F32, name="flipped", tag="bank")
+                    flipped = shared_banks.tile([P, PIECE], F32, name="flipped", tag="bank")
                     for block in range(BLOCKS):
                         columns = slice(block * BLOCK, (block + 1) * BLOCK)
-                        nc.tensor.transpose(flipped[n][:, columns], gap_f32[piece][n][:, columns], identity[:])
+                        nc.tensor.transpose(flipped[:, columns], gap_f32[piece][n][:, columns], identity[:])
+                    flipped_pair[piece][n] = flipped
+
+            for piece in range(pair * PAIR, (pair + 1) * PAIR):
+                flipped = flipped_pair[piece]
                 first = work.tile([P, PIECE], F32, name="first")
                 both = work.tile([P, PIECE], F32, name="both")
                 parts = 2 if piece == PIECES - 1 else 1

@@ -89,13 +89,13 @@ def tile_dynamicmetaembedding_kernel(tc, table, w0, w1, w2, b0, b1, b2, wa, offs
                     exact[n][:], proj[n][:], b_sb[n][:], last[:], ALU.add, ALU.subtract
                 )
                 rounded[n] = held.tile([P, PIECE], BF16, name=f"gap{n}_bf16_{piece}")
-            nc.scalar.activation(rounded[0][:], exact[0][:], FUNC.Copy)
+            nc.gpsimd.tensor_scalar(rounded[0][:], exact[0][:], 1.0, 0.0, ALU.mult, ALU.add)
             nc.vector.tensor_copy(rounded[1][:], exact[1][:])
             gap_f32.append(exact)
             gap_bf16.append(rounded)
 
-        for pair in range(PIECES // PAIR):
-            exponents = shared_banks.tile([P, PAIR * BLOCKS * EXPONENTS], F32, name="exponents", tag="bank")
+        def weigh(pair, banks, tag):
+            exponents = banks.tile([P, PAIR * BLOCKS * EXPONENTS], F32, name="exponents", tag=tag)
             for block in range(PAIR * BLOCKS):
                 piece, block_in_piece = pair * PAIR + block // BLOCKS, block % BLOCKS
                 for n in OTHERS:
@@ -106,7 +106,6 @@ def tile_dynamicmetaembedding_kernel(tc, table, w0, w1, w2, b0, b1, b2, wa, offs
                         start=(n == OTHERS[0]),
                         stop=(n == OTHERS[-1]),
                     )
-
             grown = small.tile([P, PAIR * BLOCKS * EXPONENTS], F32, name="grown")
             nc.scalar.activation(grown[:], exponents[:], FUNC.Exp)
             grown_by_weight = grown[:].rearrange("p (w t) -> p w t", t=TERMS)
@@ -116,48 +115,57 @@ def tile_dynamicmetaembedding_kernel(tc, table, w0, w1, w2, b0, b1, b2, wa, offs
             )
             attn = small.tile([P, PAIR * BLOCKS * len(OTHERS)], F32, name="attn")
             nc.vector.reciprocal(attn[:], total[:])
+            return attn
 
-            flipped_pair = {}
-            for piece in range(pair * PAIR, (pair + 1) * PAIR):
-                flipped_pair[piece] = {}
-                for n in OTHERS:
-                    flipped = shared_banks.tile([P, PIECE], F32, name="flipped", tag="bank")
-                    for block in range(BLOCKS):
-                        columns = slice(block * BLOCK, (block + 1) * BLOCK)
-                        nc.tensor.transpose(flipped[:, columns], gap_f32[piece][n][:, columns], identity[:])
-                    flipped_pair[piece][n] = flipped
-
-            for piece in range(pair * PAIR, (pair + 1) * PAIR):
-                flipped = flipped_pair[piece]
-                first = work.tile([P, PIECE], F32, name="first")
-                both = work.tile([P, PIECE], F32, name="both")
-                parts = 2 if piece == PIECES - 1 else 1
-                width = PIECE // parts
-                backs = [back_banks.tile([P, width], F32, name="back")]
-                if parts == 2:
-                    backs.append(shared_banks.tile([P, width], F32, name="back_end", tag="bank"))
+        def flip(piece):
+            flipped = []
+            for n in OTHERS:
+                bank = shared_banks.tile([P, PIECE], F32, name="flipped", tag="bank")
                 for block in range(BLOCKS):
                     columns = slice(block * BLOCK, (block + 1) * BLOCK)
-                    first_column = ((piece % PAIR) * BLOCKS + block) * len(OTHERS)
-                    weight = [attn[:, first_column + n : first_column + n + 1] for n in OTHERS]
-                    nc.scalar.activation(first[:, columns], flipped[0][:, columns], FUNC.Copy, scale=weight[0])
-                    nc.vector.scalar_tensor_tensor(
-                        both[:, columns], flipped[1][:, columns], weight[1], first[:, columns], ALU.mult, ALU.add
-                    )
-                    back, column = backs[block * BLOCK // width], block * BLOCK % width
-                    nc.tensor.transpose(back[:, column : column + BLOCK], both[:, columns], identity[:])
-                mixed = held.tile([P, PIECE], F32, name=f"mixed_{piece}")
-                if piece == 0:
-                    copied = work.tile([P, PIECE], F32, name="copied")
-                    nc.scalar.activation(copied[:], backs[0][:], FUNC.Copy)
-                    nc.gpsimd.tensor_tensor(mixed[:], copied[:], p_last[piece][:], ALU.add)
-                else:
-                    for part, back in enumerate(backs):
-                        columns = slice(part * width, (part + 1) * width)
-                        nc.vector.tensor_tensor(mixed[:, columns], back[:], p_last[piece][:, columns], ALU.add)
-                for part in range(parts):
-                    queue = (nc.sync, nc.scalar)[part]
+                    nc.tensor.transpose(bank[:, columns], gap_f32[piece][n][:, columns], identity[:])
+                flipped.append(bank)
+            return flipped
+
+        def mix(piece, flipped, attn):
+            first = work.tile([P, PIECE], F32, name="first")
+            both = work.tile([P, PIECE], F32, name="both")
+            parts = 2 if piece == PIECES - 1 else 1
+            width = PIECE // parts
+            backs = [back_banks.tile([P, width], F32, name="back", tag="back")]
+            if parts == 2:
+                backs.append(shared_banks.tile([P, width], F32, name="back_end", tag="bank"))
+            for block in range(BLOCKS):
+                columns = slice(block * BLOCK, (block + 1) * BLOCK)
+                first_column = ((piece % PAIR) * BLOCKS + block) * len(OTHERS)
+                weight = [attn[:, first_column + n : first_column + n + 1] for n in OTHERS]
+                nc.scalar.activation(first[:, columns], flipped[0][:, columns], FUNC.Copy, scale=weight[0])
+                nc.vector.scalar_tensor_tensor(
+                    both[:, columns], flipped[1][:, columns], weight[1], first[:, columns], ALU.mult, ALU.add
+                )
+                back, column = backs[block * BLOCK // width], block * BLOCK % width
+                nc.tensor.transpose(back[:, column : column + BLOCK], both[:, columns], identity[:])
+            mixed = held.tile([P, PIECE], F32, name=f"mixed_{piece}")
+            if piece == 0:
+                copied = work.tile([P, PIECE], F32, name="copied")
+                nc.scalar.activation(copied[:], backs[0][:], FUNC.Copy)
+                nc.gpsimd.tensor_tensor(mixed[:], copied[:], p_last[piece][:], ALU.add)
+            else:
+                for part, back in enumerate(backs):
                     columns = slice(part * width, (part + 1) * width)
-                    queue.dma_start(
-                        out[:, piece * PIECE + part * width : piece * PIECE + (part + 1) * width], mixed[:, columns]
-                    )
+                    nc.vector.tensor_tensor(mixed[:, columns], back[:], p_last[piece][:, columns], ALU.add)
+            for part in range(parts):
+                queue = (nc.sync, nc.scalar)[part]
+                columns = slice(part * width, (part + 1) * width)
+                queue.dma_start(
+                    out[:, piece * PIECE + part * width : piece * PIECE + (part + 1) * width], mixed[:, columns]
+                )
+
+        attn = [weigh(0, shared_banks, "bank")]
+        flipped = {piece: flip(piece) for piece in range(PIECES - 1)}
+        attn.append(weigh(1, back_banks, "back"))
+        for piece in range(PAIR):
+            mix(piece, flipped[piece], attn[0])
+        flipped[PIECES - 1] = flip(PIECES - 1)
+        for piece in range(PAIR, PIECES):
+            mix(piece, flipped[piece], attn[1])

import concourse.mybir as mybir
from concourse.masks import make_identity

BF16, F32, U16 = mybir.dt.bfloat16, mybir.dt.float32, mybir.dt.uint16
FUNC = mybir.ActivationFunctionType
ALU = mybir.AluOpType

P = 128
WORDS = 4096
TOKENS = 2048
PROJS = 3
LAST = 2
OTHERS = (0, 1)
PIECE = 512
BLOCK = 128
BLOCKS = PIECE // BLOCK
PIECES = TOKENS // PIECE
PAIR = 2
TABLE_LOADS = 2
SIGNS = ((-1.0, -1.0, 1.0, 0.0), (0.0, 1.0, -1.0, -1.0))
EXPONENTS = 4
TERMS = EXPONENTS // len(OTHERS)

FLOPS = 2 * TOKENS * PROJS * (P * P + P)


def tile_dynamicmetaembedding_kernel(tc, table, w0, w1, w2, b0, b1, b2, wa, offs, out):
    nc = tc.nc
    with (
        tc.tile_pool(name="held", bufs=1) as held,
        tc.tile_pool(name="work", bufs=2) as work,
        tc.tile_pool(name="small", bufs=2) as small,
        tc.psum_pool(name="shared_banks", bufs=6) as shared_banks,
        tc.psum_pool(name="back_banks", bufs=2) as back_banks,
    ):
        table_sb = held.tile([P, WORDS], BF16, name="table_sb")
        span = WORDS // TABLE_LOADS
        for part, queue in enumerate((nc.sync, nc.scalar)):
            queue.dma_start(
                table_sb[:, part * span : (part + 1) * span], table[:, part * span : (part + 1) * span]
            )
        offsets = held.tile([P, TOKENS // 16], U16, name="offsets")
        nc.sync.dma_start(offsets[:], offs)

        w_sb = [held.tile([P, P], BF16, name=f"w{n}_sb") for n in range(PROJS)]
        b_sb = [held.tile([P, 1], F32, name=f"b{n}_sb") for n in range(PROJS)]
        wa_sb = held.tile([P, 1], BF16, name="wa_sb")
        nc.scalar.dma_start(w_sb[LAST][:], w2)
        nc.scalar.dma_start(b_sb[LAST][:], b2)
        nc.sync.dma_start(wa_sb[:], wa)
        nc.sync.dma_start(w_sb[0][:], w0)
        nc.sync.dma_start(w_sb[1][:], w1)
        nc.sync.dma_start(b_sb[0][:], b0)
        nc.sync.dma_start(b_sb[1][:], b1)

        identity = held.tile([P, P], F32, name="identity")
        make_identity(nc, identity[:])

        zero = held.tile([P, 1], F32, name="zero")
        nc.vector.memset(zero[:], 0.0)
        one = held.tile([P, 1], F32, name="one")
        nc.scalar.activation(one[:], zero[:], FUNC.Exp)

        signs = held.tile([P, len(OTHERS) * EXPONENTS], F32, name="signs")
        for n in OTHERS:
            for e, sign in enumerate(SIGNS[n]):
                nc.vector.memset(signs[:, n * EXPONENTS + e : n * EXPONENTS + e + 1], sign)
        signed_wa = held.tile([P, len(OTHERS) * EXPONENTS], BF16, name="signed_wa")
        nc.vector.tensor_scalar_mul(signed_wa[:], signs[:], wa_sb[:])

        p_last, gap_f32, gap_bf16 = [], [], []
        for piece in range(PIECES):
            piece_offsets = offsets[:, piece * (PIECE // 16) : (piece + 1) * (PIECE // 16)]
            proj = {}
            for n in (LAST,) + OTHERS:
                proj[n] = shared_banks.tile([P, PIECE], F32, name="proj", tag="bank")
                nc.tensor.matmul(
                    proj[n][:], w_sb[n][:], table_sb[:].indirect(piece_offsets), start=True, stop=True
                )

            last = held.tile([P, PIECE], F32, name=f"p_last_{piece}")
            nc.scalar.activation(last[:], proj[LAST][:], FUNC.Identity, bias=b_sb[LAST][:])
            p_last.append(last)

            exact, rounded = {}, {}
            for n in OTHERS:
                exact[n] = held.tile([P, PIECE], F32, name=f"gap{n}_f32_{piece}")
                nc.vector.scalar_tensor_tensor(
                    exact[n][:], proj[n][:], b_sb[n][:], last[:], ALU.add, ALU.subtract
                )
                rounded[n] = held.tile([P, PIECE], BF16, name=f"gap{n}_bf16_{piece}")
            nc.gpsimd.tensor_scalar(rounded[0][:], exact[0][:], 1.0, 0.0, ALU.mult, ALU.add)
            nc.vector.tensor_copy(rounded[1][:], exact[1][:])
            gap_f32.append(exact)
            gap_bf16.append(rounded)

        def weigh(pair, banks, tag):
            exponents = banks.tile([P, PAIR * BLOCKS * EXPONENTS], F32, name="exponents", tag=tag)
            for block in range(PAIR * BLOCKS):
                piece, block_in_piece = pair * PAIR + block // BLOCKS, block % BLOCKS
                for n in OTHERS:
                    nc.tensor.matmul(
                        exponents[:, block * EXPONENTS : (block + 1) * EXPONENTS],
                        gap_bf16[piece][n][:, block_in_piece * BLOCK : (block_in_piece + 1) * BLOCK],
                        signed_wa[:, n * EXPONENTS : (n + 1) * EXPONENTS],
                        start=(n == OTHERS[0]),
                        stop=(n == OTHERS[-1]),
                    )
            grown = small.tile([P, PAIR * BLOCKS * EXPONENTS], F32, name="grown")
            nc.scalar.activation(grown[:], exponents[:], FUNC.Exp)
            grown_by_weight = grown[:].rearrange("p (w t) -> p w t", t=TERMS)
            total = small.tile([P, PAIR * BLOCKS * len(OTHERS)], F32, name="total")
            nc.vector.scalar_tensor_tensor(
                total[:].unsqueeze(2), grown_by_weight[:, :, 0:1], 1.0, grown_by_weight[:, :, 1:2], ALU.add, ALU.add
            )
            attn = small.tile([P, PAIR * BLOCKS * len(OTHERS)], F32, name="attn")
            nc.vector.reciprocal(attn[:], total[:])
            return attn

        def flip(piece):
            flipped = []
            for n in OTHERS:
                bank = shared_banks.tile([P, PIECE], F32, name="flipped", tag="bank")
                for block in range(BLOCKS):
                    columns = slice(block * BLOCK, (block + 1) * BLOCK)
                    nc.tensor.transpose(bank[:, columns], gap_f32[piece][n][:, columns], identity[:])
                flipped.append(bank)
            return flipped

        def mix(piece, flipped, attn):
            first = work.tile([P, PIECE], F32, name="first")
            both = work.tile([P, PIECE], F32, name="both")
            parts = 2 if piece == PIECES - 1 else 1
            width = PIECE // parts
            backs = [back_banks.tile([P, width], F32, name="back", tag="back")]
            if parts == 2:
                backs.append(shared_banks.tile([P, width], F32, name="back_end", tag="bank"))
            for block in range(BLOCKS):
                columns = slice(block * BLOCK, (block + 1) * BLOCK)
                first_column = ((piece % PAIR) * BLOCKS + block) * len(OTHERS)
                weight = [attn[:, first_column + n : first_column + n + 1] for n in OTHERS]
                nc.scalar.activation(first[:, columns], flipped[0][:, columns], FUNC.Copy, scale=weight[0])
                nc.vector.scalar_tensor_tensor(
                    both[:, columns], flipped[1][:, columns], weight[1], first[:, columns], ALU.mult, ALU.add
                )
                back, column = backs[block * BLOCK // width], block * BLOCK % width
                nc.tensor.transpose(back[:, column : column + BLOCK], both[:, columns], identity[:])
            mixed = held.tile([P, PIECE], F32, name=f"mixed_{piece}")
            if piece == 0:
                copied = work.tile([P, PIECE], F32, name="copied")
                nc.scalar.activation(copied[:], backs[0][:], FUNC.Copy)
                nc.gpsimd.tensor_tensor(mixed[:], copied[:], p_last[piece][:], ALU.add)
            else:
                for part, back in enumerate(backs):
                    columns = slice(part * width, (part + 1) * width)
                    nc.vector.tensor_tensor(mixed[:, columns], back[:], p_last[piece][:, columns], ALU.add)
            for part in range(parts):
                queue = (nc.sync, nc.scalar)[part]
                columns = slice(part * width, (part + 1) * width)
                queue.dma_start(
                    out[:, piece * PIECE + part * width : piece * PIECE + (part + 1) * width], mixed[:, columns]
                )

        attn = [weigh(0, shared_banks, "bank")]
        flipped = {piece: flip(piece) for piece in range(PIECES - 1)}
        attn.append(weigh(1, back_banks, "back"))
        for piece in range(PAIR):
            mix(piece, flipped[piece], attn[0])
        flipped[PIECES - 1] = flip(PIECES - 1)
        for piece in range(PAIR, PIECES):
            mix(piece, flipped[piece], attn[1])
